import numpy as np
import ml_dtypes


def mxq(x, axis, fmt="e4m3"):
    dtype, down = {"e4m3": (ml_dtypes.float8_e4m3fn, 7), "e5m2": (ml_dtypes.float8_e5m2, 14)}[fmt]
    v = np.moveaxis(np.asarray(x, np.float32).astype(ml_dtypes.bfloat16).astype(np.float64), axis, -1)
    blocks = v.reshape(v.shape[:-1] + (-1, 32))
    amax = np.abs(blocks).max(-1, keepdims=True)
    byte = np.maximum(np.where(amax > 0, np.frexp(amax)[1] - 1 + 127, 0) - down, 1)
    scale = np.exp2(byte - 127.0)
    codes = (blocks / scale).astype(np.float32).astype(dtype).astype(np.float64)
    return np.moveaxis((codes * scale).reshape(v.shape), -1, axis)


WIDE = False


def mx_kscale(k):
    if not WIDE:
        return np.ones(k)
    levels = np.array([10, -10, 5, -5, 0])
    if k % 512:
        return np.exp2(np.random.permutation(np.resize(levels, k // 32))).repeat(32)
    a = np.empty((k // 512, 16))
    for p in range(k // 512):
        a[p, :8] = np.random.permutation(np.resize(levels, 8))
        for g in range(8):
            far = levels[np.abs(levels - a[p, g]) >= 10]
            a[p, g + 8] = far[np.random.randint(len(far))]
    return np.exp2(a.ravel()).repeat(32)


BF16 = ml_dtypes.bfloat16


def bf(x):
    return np.asarray(x, np.float32).astype(BF16)


def f64(x):
    return np.asarray(x).astype(np.float64)


B, S, HID, NH, HD, RD, KVC, QC = 2, 1024, 8192, 16, 128, 64, 2048, 6144


def heads(t, d):
    return t.reshape(B, S, NH, d).transpose(0, 2, 1, 3)


def rope(t):
    R = t.shape[-1]
    inv_freq = 1.0 / (10000.0 ** (np.arange(0, R, 2) / R))
    ang = np.arange(t.shape[-2])[:, None] * inv_freq[None, :]
    cos, sin = np.cos(ang), np.sin(ang)
    t1, t2 = t[..., : R // 2], t[..., R // 2:]
    return np.concatenate([t1 * cos - t2 * sin, t2 * cos + t1 * sin], axis=-1)


def setup_inputs():
    s, t = mx_kscale(HID), mx_kscale(KVC)
    return {"x": bf(np.random.standard_normal((B, S, HID)) * s),
            "W_kvd": bf(np.random.standard_normal((HID, KVC)) / np.sqrt(HID) / s[:, None] * t),
            "b_kvd": bf(np.random.standard_normal(KVC) * 0.3 * t),
            "W_ku": bf(np.random.standard_normal((KVC, NH * HD)) / np.sqrt(KVC) / t[:, None]),
            "b_ku": bf(np.random.standard_normal(NH * HD) * 0.3),
            "W_vu": bf(np.random.standard_normal((KVC, NH * HD)) / np.sqrt(KVC) / t[:, None]),
            "b_vu": bf(np.random.standard_normal(NH * HD) * 0.3),
            "W_kr": bf(np.random.standard_normal((KVC, NH * RD)) / np.sqrt(KVC) / t[:, None]),
            "b_kr": bf(np.random.standard_normal(NH * RD) * 0.3)}


def reference(x, W_kvd, b_kvd, W_ku, b_ku, W_vu, b_vu, W_kr, b_kr):
    kv_c = (mxq(f64(x), 2, "e4m3") @ mxq(f64(W_kvd), 0, "e4m3")) + f64(b_kvd)
    cq = mxq(kv_c, 2, "e4m3")
    keys_c = heads((cq @ mxq(f64(W_ku), 0, "e4m3")) + f64(b_ku), HD)
    values = heads((cq @ mxq(f64(W_vu), 0, "e4m3")) + f64(b_vu), HD)
    keys_r = rope(heads((cq @ mxq(f64(W_kr), 0, "e4m3")) + f64(b_kr), RD))
    return np.concatenate([keys_c, keys_r], axis=-1), values

@@ -1,0 +1,491 @@
+from contextlib import ExitStack
+import math
+
+import concourse.mybir as mybir
+from concourse.masks import make_identity
+
+F32 = mybir.dt.float32
+BF16 = mybir.dt.bfloat16
+U32 = mybir.dt.uint32
+U8 = mybir.dt.uint8
+I32 = mybir.dt.int32
+FP8 = mybir.dt.float8_e4m3fn_x4
+ALU = mybir.AluOpType
+ACT = mybir.ActivationFunctionType
+
+FLOPS = 2 * 2048 * 8192 * 2048 + 2 * 2048 * 2048 * 5120
+
+P = 128
+PI = 3.141592653589793
+NG = 4
+NRAW = 3
+EARLY = 30
+LATE_EVERY = 2
+FIRST = 8
+
+
+def turn_constants():
+    heads, rests = [], []
+    for j in range(32):
+        f = math.exp(-math.log(10000.0) * j / 32.0) / (2.0 * PI)
+        s = 0
+        for i in range(40):
+            if f * (2.0 ** s) < 2048.0:
+                s = s + 1
+        head = int(f * (2.0 ** s)) / (2.0 ** s)
+        heads.append(head)
+        rests.append(f - head)
+    return heads, rests
+
+
+def tile_multiheadlatentattention_pa_l_kernel(
+    tc, x, W_kvd, b_kvd, W_ku, b_ku, W_vu, b_vu, W_kr, b_kr, out_0, out_1
+):
+    nc = tc.nc
+    xf = x.flatten_outer_dims()
+    with ExitStack() as ctx:
+        sb = ctx.enter_context(tc.tile_pool(name="sb", bufs=1))
+        ps = ctx.enter_context(tc.psum_pool(name="ps", bufs=1))
+        ctx.enter_context(tc.manual_schedule())
+
+        def sbt(shape, dtype, tag, label):
+            return sb.tile(shape, dtype, name=label, tag=tag, align_bytes=64)
+
+        def bank(b, shape, label):
+            return ps.tile(shape, F32, name=label, tag="bank%d" % b)
+
+        st = {"gx": 0, "gw": 0, "dma": 0, "ic": 0, "q": 0, "bank": 4, "tile": 0}
+
+        def granule(kind, label):
+            i = st[kind] % NG
+            st[kind] = st[kind] + 1
+            return sbt([P, 1024], BF16, "%s%d" % (kind, i), label)
+
+        xraw, tpb, xg, xcu, xpu = {}, {}, {}, {}, {}
+
+        def load_x(n):
+            tb, j = divmod(n, 8)
+            tag = ("cc1", "cc2", "xc6", "xc7")[n % 4] if n < 8 else "cc%d" % (1 + n % 2)
+            t = sbt([P, 4, 1024], BF16, tag, "xraw%d" % n)
+            src = xf[tb * 512 : (tb + 1) * 512, j * 1024 : (j + 1) * 1024].rearrange("(a p) k -> p a k", p=P)
+            if n == 0:
+                for a in range(4):
+                    nc.sync.dma_start(out=t[:, a, :], in_=src[:, a, :])
+            else:
+                nc.sync.dma_start(out=t, in_=src)
+            xraw[n] = t
+
+        def transposes(n):
+            words = xraw[n].rearrange("p a k -> p (a k)").bitcast(F32)
+            for kl in range(2):
+                for h in range(2):
+                    b = bank(4 + 2 * kl + h, [P, 2, 2, P], "tp%d_%d%d" % (n, kl, h))
+                    tpb[(n, kl, h)] = b
+                    for a2 in range(2):
+                        for u in range(2):
+                            base = (2 * h + a2) * 512 + kl * 256 + u
+                            nc.tensor.transpose(b[:, a2, u, :], words[:, base : base + 255 : 2], ident)
+
+        def copy_out(n, kl, h, eng):
+            g = granule("gx", "xg%d_%d%d" % (n, kl, h))
+            dst = g.bitcast(F32).rearrange("p (a r u) -> p a r u", a=2, u=2)
+            src = tpb[(n, kl, h)].rearrange("p a u r -> p a r u")
+            if eng == "v":
+                nc.vector.tensor_copy(out=dst, in_=src)
+            else:
+                nc.scalar.copy(out=dst, in_=src)
+            xg[(n, kl, h)] = g
+
+        def quant_x(n, kl, h):
+            tb, j = divmod(n, 8)
+            kp = 2 * j + kl
+            i, r = tb * 4 + kp // 4, kp % 4
+            if i not in xcu:
+                xcu[i] = sbt([P, 4, 512], U32, "xc%d" % i, "xcodes%d" % i)
+                xpu[i] = sbt([P, 512], U8, "xp%d" % i, "xplane%d" % i)
+            cols = slice(h * 256, (h + 1) * 256)
+            nc.vector.quantize_mx(
+                out=xcu[i][:, r, cols].bitcast(FP8), scales=xpu[i][4 * r : P, cols], in_=xg[(n, kl, h)]
+            )
+
+        jobs = []
+        for U in range(16):
+            for r in range(4):
+                kp = 4 * (U % 4) + r
+                g = U // 4
+                jobs.append(("w", U, r, W_kvd[kp * 512 : (kp + 1) * 512, g * 512 : (g + 1) * 512]))
+        for i in range(10):
+            if i < 4:
+                src, c0 = W_vu, i
+            elif i < 8:
+                src, c0 = W_ku, i - 4
+            else:
+                src, c0 = W_kr, i - 8
+            for r in range(4):
+                jobs.append(("u", i, r, src[r * 512 : (r + 1) * 512, c0 * 512 : (c0 + 1) * 512]))
+        wraw, wg, units, wpair = {}, {}, {}, {}
+
+        def job_dma():
+            k = st["dma"]
+            if k >= len(jobs):
+                return
+            st["dma"] = k + 1
+            if k < 16:
+                if k % 2 == 0:
+                    wpair[k // 2] = sbt([P, 2, 4, 512], BF16, "xc%d" % (8 + k // 2), "rawpair%d" % (k // 2))
+                t = wpair[k // 2][:, k % 2]
+            else:
+                t = sbt([P, 4, 512], BF16, "raw%d" % (k % NRAW), "raw_j%d" % k)
+            nc.sync.dma_start(out=t, in_=jobs[k][3].rearrange("(p j) c -> p j c", j=4))
+            wraw[k] = t
+
+        def job_ic(k, engs):
+            kind = jobs[k][0]
+            for h in range(2):
+                g = granule("gw", "wg%d_%d" % (k, h))
+                if kind == "w":
+                    src = wraw[k].rearrange("p j (m t) -> p t m j", t=4)[:, 2 * h : 2 * h + 2]
+                    dst = g.rearrange("p (t m j) -> p t m j", t=2, j=4)
+                else:
+                    src = wraw[k][:, :, h * 256 : (h + 1) * 256].rearrange("p j c -> p c j")
+                    dst = g.rearrange("p (c j) -> p c j", j=4)
+                if engs[h] == "v":
+                    nc.vector.tensor_copy(out=dst, in_=src)
+                else:
+                    nc.scalar.copy(out=dst, in_=src)
+                wg[(k, h)] = g
+
+        def job_q(k):
+            kind, U, r = jobs[k][0], jobs[k][1], jobs[k][2]
+            if r == 0:
+                if kind == "w":
+                    units[(kind, U)] = (
+                        sbt([P, 4, 512], U32, "wc%d" % (U % 5), "wcodes%d" % U),
+                        sbt([P, 512], U8, "wp%d" % (U % 5), "wplane%d" % U),
+                    )
+                else:
+                    units[(kind, U)] = (
+                        sbt([P, 4, 512], U32, "xc%d" % U, "ucodes%d" % U),
+                        sbt([P, 512], U8, "xp%d" % U, "uplane%d" % U),
+                    )
+            codes, plane = units[(kind, U)]
+            for h in range(2):
+                cols = slice(h * 256, (h + 1) * 256)
+                nc.vector.quantize_mx(
+                    out=codes[:, r, cols].bitcast(FP8), scales=plane[4 * r : P, cols], in_=wg[(k, h)]
+                )
+
+        def flush_q():
+            if st["q"] < st["ic"]:
+                job_q(st["q"])
+                st["q"] = st["q"] + 1
+
+        def advance(engs):
+            k = st["ic"]
+            if k >= len(jobs):
+                flush_q()
+                return
+            job_ic(k, engs)
+            st["ic"] = k + 1
+            if st["q"] < k:
+                flush_q()
+            if st["dma"] <= k + NRAW:
+                job_dma()
+
+        when = []
+        for U in range(16):
+            for r in range(4):
+                if U == 0:
+                    when.append(-1)
+                elif U < 4:
+                    when.append((4 * U + r - 4) // 2)
+                elif U % 4 == 0:
+                    when.append((U // 4 - 1) * 32 + 8 + 2 * r)
+                else:
+                    V = U - 5
+                    when.append((V // 4) * 32 + 24 + 2 * (V % 4) + 2 + r // 2)
+        for m in range(40):
+            when.append(98 + m if m < EARLY else 1000)
+
+        def run_jobs(sig, engs, most):
+            did = 0
+            for i in range(most):
+                if st["ic"] < len(jobs) and when[st["ic"]] <= sig:
+                    advance(engs)
+                    did = did + 1
+            return did
+
+        acc, cc, cwork = {}, {}, []
+
+        def mm1(sig):
+            g, r = divmod(sig, 32)
+            tb, j = divmod(r, 8)
+            s = g * 4 + tb
+            base = 0 if g == 0 else 4 * ((s + 1) % 2)
+            if j == 0:
+                for t in range(4):
+                    acc[t] = bank(base + t, [P, 512], "acc%d_%d" % (s, t))
+            for kl in range(2):
+                kp = 2 * j + kl
+                q, rr = kp // 4, kp % 4
+                assert st["q"] >= 4 * (4 * g + q) + 4
+                codes, plane = units[("w", 4 * g + q)]
+                for t in range(4):
+                    cols = slice(t * P, (t + 1) * P)
+                    nc.tensor.matmul_mx(
+                        out=acc[t],
+                        lhsT=codes[:, rr, cols].bitcast(FP8),
+                        lhsT_scale=plane[4 * rr : P, cols],
+                        rhs=xcu[tb * 4 + q][:, rr, :].bitcast(FP8),
+                        rhs_scale=xpu[tb * 4 + q][4 * rr : P, :],
+                        start=(kp == 0),
+                        stop=(kp == 15),
+                    )
+
+        def evac(g, tb):
+            cbf = sbt([P, 4, 512], BF16, "cbf", "cbf%d_%d" % (g, tb))
+            for t in range(4):
+                col = bk[:, 4 * g + t : 4 * g + t + 1]
+                if t % 2 == 0:
+                    nc.scalar.activation(out=cbf[:, t, :], in_=acc[t], func=ACT.Identity, bias=col, scale=1.0)
+                else:
+                    nc.vector.tensor_scalar(out=cbf[:, t, :], in0=acc[t], scalar1=col, scalar2=None, op0=ALU.add)
+            cwork.append((g, tb, cbf))
+
+        def c_quant():
+            if len(cwork) == 0:
+                return
+            flush_q()
+            g, tb, cbf = cwork.pop(0)
+            if tb == 0:
+                cc[g] = sbt([P, 2048], U32, ("cc%d" % g) if g < 3 else "wc1", "ccodes%d" % g)
+            gs = []
+            for h in range(2):
+                gr = granule("gw", "cg%d_%d_%d" % (g, tb, h))
+                nc.vector.tensor_copy(
+                    out=gr.rearrange("p (n t) -> p n t", t=4),
+                    in_=cbf[:, :, h * 256 : (h + 1) * 256].rearrange("p t n -> p n t"),
+                )
+                gs.append(gr)
+            for h in range(2):
+                cols = slice(tb * 512 + h * 256, tb * 512 + (h + 1) * 256)
+                nc.vector.quantize_mx(out=cc[g][:, cols].bitcast(FP8), scales=cp[4 * g : P, cols], in_=gs[h])
+
+        tabs = {}
+
+        def rope_part1():
+            tmp = sbt([P, 2048], F32, "cc2", "ropetmp")
+            tabs["tmp"] = tmp
+            posi = tmp[:, 2040:2048].bitcast(I32)
+            posf = tmp[:, 2032:2040]
+            nc.gpsimd.iota(posi, pattern=[[128, 8]], base=0, channel_multiplier=1)
+            nc.vector.tensor_copy(out=posf, in_=posi)
+            heads, rests = turn_constants()
+            th = tmp[:, 0:256].rearrange("p (s j) -> p s j", j=32)
+            tl = tmp[:, 256:512].rearrange("p (s j) -> p s j", j=32)
+            for j in range(32):
+                nc.gpsimd.tensor_scalar(
+                    out=th[:, :, j], in0=posf, scalar1=heads[j], scalar2=0.0, op0=ALU.mult, op1=ALU.add
+                )
+                nc.gpsimd.tensor_scalar(
+                    out=tl[:, :, j], in0=posf, scalar1=rests[j], scalar2=0.0, op0=ALU.mult, op1=ALU.add
+                )
+
+        def rope_part2():
+            tmp = tabs["tmp"]
+            th, tl = tmp[:, 0:256], tmp[:, 256:512]
+            ni = tmp[:, 512:768].bitcast(I32)
+            nf, r1, r2, rc = [tmp[:, 768 + 256 * i : 1024 + 256 * i] for i in range(4)]
+            ws, wc = th, tl
+            nc.vector.tensor_copy(out=ni, in_=th)
+            nc.vector.tensor_copy(out=nf, in_=ni)
+            nc.vector.tensor_tensor(out=r1, in0=th, in1=nf, op=ALU.subtract)
+            nc.vector.tensor_tensor(out=r2, in0=r1, in1=tl, op=ALU.add)
+            nc.vector.tensor_scalar(out=rc, in0=r2, scalar1=0.25, scalar2=None, op0=ALU.add)
+            nc.vector.scalar_tensor_tensor(out=ws, in0=r2, scalar=0.5, in1=r2, op0=ALU.is_gt, op1=ALU.subtract)
+            nc.vector.scalar_tensor_tensor(out=wc, in0=rc, scalar=0.5, in1=rc, op0=ALU.is_gt, op1=ALU.subtract)
+            tab = sbt([P, 512], F32, "gx0", "ropetab")
+            tabs["sin"], tabs["cos"] = tab[:, 0:256], tab[:, 256:512]
+            nc.scalar.activation(out=tabs["sin"], in_=ws, func=ACT.Sin, scale=-2.0 * PI)
+            nc.scalar.activation(out=tabs["cos"], in_=wc, func=ACT.Sin, scale=-2.0 * PI)
+
+        ident = sbt([P, P], F32, "ident", "ident")
+        make_identity(nc, ident)
+        bkb = sbt([P, 4, 4], BF16, "bkb", "bkb")
+        bk = sbt([P, 16], F32, "bk", "bk")
+        cp = sbt([P, 2048], U8, "cp", "cplane")
+
+        def x_front(n, nv):
+            transposes(n)
+            for i in range(4):
+                copy_out(n, i // 2, i % 2, "v" if i < nv else "s")
+
+        def x_back(n):
+            for i in (3, 0, 2, 1):
+                quant_x(n, i // 2, i % 2)
+
+        for n in range(4):
+            load_x(n)
+            job_dma()
+            job_dma()
+        nc.sync.dma_start(out=bkb, in_=b_kvd.rearrange("(g p t) -> p g t", p=P, t=4))
+        x_front(0, 1)
+        advance("vs")
+        advance("vs")
+        x_back(0)
+        x_front(1, 1)
+        advance("vs")
+        advance("vs")
+        x_back(1)
+        flush_q()
+        nc.vector.tensor_copy(out=bk, in_=bkb.rearrange("p g t -> p (g t)"))
+
+        for sig in range(128):
+            if sig + 2 < 32:
+                x_front(sig + 2, 1 if (sig < 8 or sig >= 24) else 2)
+                if sig + 4 < 32:
+                    load_x(sig + 4)
+                if sig < 4:
+                    job_dma()
+                    job_dma()
+            did = run_jobs(sig, "vs", 1)
+            if sig + 2 < 32:
+                x_back(sig + 2)
+            did = did + run_jobs(sig, "vs", 8)
+            if did == 0:
+                flush_q()
+            c_quant()
+            if sig == 33:
+                rope_part1()
+            if sig == 46:
+                rope_part2()
+            if sig == 120:
+                bkv = sbt([P, 4096], BF16, "xc10", "bias_kv")
+                bkr = sbt([P, 1024], BF16, "xc11", "bias_kr")
+                nc.sync.dma_start(out=bkr, in_=b_kr.partition_broadcast(P))
+                nc.sync.dma_start(out=bkv[:, 0:2048], in_=b_ku.partition_broadcast(P))
+                nc.sync.dma_start(out=bkv[:, 2048:4096], in_=b_vu.partition_broadcast(P))
+            mm1(sig)
+            if sig % 8 == 7:
+                evac(sig // 32, (sig % 32) // 8)
+        c_quant()
+
+        def mm2(tt, i):
+            b = st["bank"] % 8
+            st["bank"] = st["bank"] + 1
+            out = bank(b, [P, 512], "o%d_%d" % (tt, i))
+            assert st["q"] >= 64 + 4 * i + 4
+            codes, plane = units[("u", i)]
+            cols = slice(tt * P, (tt + 1) * P)
+            for r in range(4):
+                nc.tensor.matmul_mx(
+                    out=out,
+                    lhsT=cc[r][:, cols].bitcast(FP8),
+                    lhsT_scale=cp[4 * r : P, cols],
+                    rhs=codes[:, r, :].bitcast(FP8),
+                    rhs_scale=plane[4 * r : P, :],
+                    start=(r == 0),
+                    stop=(r == 3),
+                )
+            return out
+
+        cos3 = tabs["cos"].rearrange("p (s j) -> p s j", j=32)
+        sin3 = tabs["sin"].rearrange("p (s j) -> p s j", j=32)
+        o0t, o1t, rot = {}, {}, {}
+
+        def late_jobs():
+            st["tile"] = st["tile"] + 1
+            if st["tile"] % LATE_EVERY == 0:
+                advance("ss")
+
+        def need(i):
+            for n in range(48):
+                if st["q"] < 64 + 4 * i + 4:
+                    advance("ss")
+
+        def kr_tiles(tt):
+            si = tt % 8
+            y = sbt([P, 16, 2, 32], F32, "wc%d" % (2 + tt % 2), "y%d" % tt)
+            for i in range(2):
+                need(8 + i)
+                o = mm2(tt, 8 + i)
+                nc.vector.tensor_tensor(
+                    out=y[:, 8 * i : 8 * i + 8].rearrange("p h f j -> p h (f j)"),
+                    in0=o.rearrange("p (h d) -> p h d", h=8),
+                    in1=bkr[:, i * 512 : (i + 1) * 512].rearrange("p (h d) -> p h d", h=8),
+                    op=ALU.add,
+                )
+                late_jobs()
+            ya = sbt([P, 32, 2, 16], F32, "raw0" if tt % 2 == 0 else "raw2", "ycos%d" % tt)
+            yb = sbt([P, 32, 2, 16], F32, "raw1" if tt % 2 == 0 else "cbf", "ysin%d" % tt)
+            yv = y.rearrange("p h f j -> p j f h")
+            for j in range(32):
+                nc.scalar.activation(out=ya[:, j], in_=yv[:, j], func=ACT.Copy, scale=cos3[:, si, j : j + 1])
+                nc.scalar.activation(out=yb[:, j], in_=yv[:, j], func=ACT.Copy, scale=sin3[:, si, j : j + 1])
+            rot[tt] = (ya.rearrange("p j f h -> p f h j"), yb.rearrange("p j f h -> p f h j"))
+
+        def rope_sum(tt, hh):
+            ya, yb = rot[tt]
+            t0 = o0t[(tt, hh)]
+            hs = slice(8 * hh, 8 * hh + 8)
+            nc.vector.tensor_tensor(out=t0[:, :, 128:160], in0=ya[:, 0, hs, :], in1=yb[:, 1, hs, :], op=ALU.subtract)
+            nc.vector.tensor_tensor(out=t0[:, :, 160:192], in0=ya[:, 1, hs, :], in1=yb[:, 0, hs, :], op=ALU.add)
+
+        def ku_tiles(tt):
+            bi, si = divmod(tt, 8)
+            rows = slice(si * P, (si + 1) * P)
+            for i in range(4):
+                hh = i // 2
+                if i % 2 == 0:
+                    o0t[(tt, hh)] = sbt([P, 8, 192], F32, "xc%d" % (12 + 2 * (tt % 2) + hh), "o0_%d_%d" % (tt, hh))
+                need(4 + i)
+                o = mm2(tt, 4 + i)
+                h0 = (i % 2) * 4
+                nc.vector.tensor_tensor(
+                    out=o0t[(tt, hh)][:, h0 : h0 + 4, 0:128],
+                    in0=o.rearrange("p (h d) -> p h d", h=4),
+                    in1=bkv[:, i * 512 : (i + 1) * 512].rearrange("p (h d) -> p h d", h=4),
+                    op=ALU.add,
+                )
+                if i % 2 == 1:
+                    rope_sum(tt, hh)
+                    nc.sync.dma_start(
+                        out=out_0[bi, 8 * hh : 8 * hh + 8, rows, :].rearrange("h s d -> s h d"), in_=o0t[(tt, hh)]
+                    )
+                late_jobs()
+
+        def vu_tile(tt, i):
+            bi, si = divmod(tt, 8)
+            rows = slice(si * P, (si + 1) * P)
+            if i == 0:
+                o1t[tt] = sbt([P, 16, 128], F32, "wc%d" % (0 if tt % 2 == 0 else 4), "o1_%d" % tt)
+            o1 = o1t[tt]
+            need(i)
+            o = mm2(tt, i)
+            nc.vector.tensor_tensor(
+                out=o1[:, 4 * i : 4 * i + 4, :],
+                in0=o.rearrange("p (h d) -> p h d", h=4),
+                in1=bkv[:, 2048 + i * 512 : 2048 + (i + 1) * 512].rearrange("p (h d) -> p h d", h=4),
+                op=ALU.add,
+            )
+            if tt == 15:
+                nc.sync.dma_start(
+                    out=out_1[bi, 4 * i : 4 * i + 4, rows, :].rearrange("h s d -> s h d"),
+                    in_=o1[:, 4 * i : 4 * i + 4, :],
+                )
+            elif i == 3:
+                nc.sync.dma_start(out=out_1[bi, :, rows, :].rearrange("h s d -> s h d"), in_=o1)
+            late_jobs()
+
+        for tt in range(FIRST):
+            for i in range(4):
+                vu_tile(tt, i)
+        rest = [(tt, i) for tt in range(FIRST, 16) for i in range(4)]
+        kr_tiles(0)
+        for n in range(16):
+            ku_tiles(n)
+            if n + 1 < 16:
+                kr_tiles(n + 1)
+            for m in range(((n + 1) * (16 - FIRST)) // 4 - (n * (16 - FIRST)) // 4):
+                tt, i = rest.pop(0)
+                vu_tile(tt, i)

@@ -19,6 +19,8 @@ P = 128
 PI = 3.141592653589793
 NG = 4
 NRAW = 3
+SORT_LO, SORT_HI = 40, 40
+NV_MID = 2
 EARLY = 30
 LATE_EVERY = 2
 FIRST = 8
@@ -61,7 +63,7 @@ def tile_multiheadlatentattention_pa_l_kernel(
             st[kind] = st[kind] + 1
             return sbt([P, 1024], BF16, "%s%d" % (kind, i), label)
 
-        xraw, tpb, xg, xcu, xpu = {}, {}, {}, {}, {}
+        xraw, tpb, xg, xcu, xpu, xsorted = {}, {}, {}, {}, {}, {}
 
         def load_x(n):
             tb, j = divmod(n, 8)
@@ -75,6 +77,12 @@ def tile_multiheadlatentattention_pa_l_kernel(
                 nc.sync.dma_start(out=t, in_=src)
             xraw[n] = t
 
+        def sort_x(n):
+            t = sbt([P, 8, 2, P], F32, "xc%d" % (12 + n % 4), "xsort%d" % n)
+            words = xraw[n].rearrange("p a k -> p (a k)").bitcast(F32)
+            nc.scalar.copy(out=t, in_=words.rearrange("p (b w u) -> p b u w", b=8, u=2))
+            xsorted[n] = t
+
         def transposes(n):
             words = xraw[n].rearrange("p a k -> p (a k)").bitcast(F32)
             for kl in range(2):
@@ -83,8 +91,11 @@ def tile_multiheadlatentattention_pa_l_kernel(
                     tpb[(n, kl, h)] = b
                     for a2 in range(2):
                         for u in range(2):
-                            base = (2 * h + a2) * 512 + kl * 256 + u
-                            nc.tensor.transpose(b[:, a2, u, :], words[:, base : base + 255 : 2], ident)
+                            if n in xsorted:
+                                nc.tensor.transpose(b[:, a2, u, :], xsorted[n][:, (2 * h + a2) * 2 + kl, u, :], ident)
+                            else:
+                                base = (2 * h + a2) * 512 + kl * 256 + u
+                                nc.tensor.transpose(b[:, a2, u, :], words[:, base : base + 255 : 2], ident)
 
         def copy_out(n, kl, h, eng):
             g = granule("gx", "xg%d_%d%d" % (n, kl, h))
@@ -338,23 +349,27 @@ def tile_multiheadlatentattention_pa_l_kernel(
         advance("vs")
         x_back(1)
         flush_q()
-        nc.vector.tensor_copy(out=bk, in_=bkb.rearrange("p g t -> p (g t)"))
 
         for sig in range(128):
             if sig + 2 < 32:
-                x_front(sig + 2, 1 if (sig < 8 or sig >= 24) else 2)
-                if sig + 4 < 32:
-                    load_x(sig + 4)
+                if SORT_LO <= sig + 3 < SORT_HI:
+                    sort_x(sig + 3)
+                x_front(sig + 2, 1 if (sig < 8 or sig >= 24) else NV_MID)
+                for n in range(4, 32):
+                    if (n - 5 if (SORT_LO <= n - 2 < SORT_HI or n in (8, 9)) else n - 4) == sig:
+                        load_x(n)
                 if sig < 4:
                     job_dma()
                     job_dma()
-            did = run_jobs(sig, "vs", 1)
+            if sig < 28:
+                run_jobs(sig, "vs", 1)
             if sig + 2 < 32:
                 x_back(sig + 2)
-            did = did + run_jobs(sig, "vs", 8)
-            if did == 0:
-                flush_q()
+            run_jobs(sig, "vs", 8)
             c_quant()
+            flush_q()
+            if sig == 5:
+                nc.vector.tensor_copy(out=bk, in_=bkb.rearrange("p g t -> p (g t)"))
             if sig == 33:
                 rope_part1()
             if sig == 46:
@@ -391,7 +406,7 @@ def tile_multiheadlatentattention_pa_l_kernel(
 
         cos3 = tabs["cos"].rearrange("p (s j) -> p s j", j=32)
         sin3 = tabs["sin"].rearrange("p (s j) -> p s j", j=32)
-        o0t, o1t, rot = {}, {}, {}
+        o0t, o1t = {}, {}
 
         def late_jobs():
             st["tile"] = st["tile"] + 1
@@ -422,22 +437,22 @@ def tile_multiheadlatentattention_pa_l_kernel(
             for j in range(32):
                 nc.scalar.activation(out=ya[:, j], in_=yv[:, j], func=ACT.Copy, scale=cos3[:, si, j : j + 1])
                 nc.scalar.activation(out=yb[:, j], in_=yv[:, j], func=ACT.Copy, scale=sin3[:, si, j : j + 1])
-            rot[tt] = (ya.rearrange("p j f h -> p f h j"), yb.rearrange("p j f h -> p f h j"))
-
-        def rope_sum(tt, hh):
-            ya, yb = rot[tt]
-            t0 = o0t[(tt, hh)]
-            hs = slice(8 * hh, 8 * hh + 8)
-            nc.vector.tensor_tensor(out=t0[:, :, 128:160], in0=ya[:, 0, hs, :], in1=yb[:, 1, hs, :], op=ALU.subtract)
-            nc.vector.tensor_tensor(out=t0[:, :, 160:192], in0=ya[:, 1, hs, :], in1=yb[:, 0, hs, :], op=ALU.add)
+            ya = ya.rearrange("p j f h -> p f h j")
+            yb = yb.rearrange("p j f h -> p f h j")
+            for hh in range(2):
+                t0 = sbt([P, 8, 192], F32, "xc%d" % (12 + 2 * (tt % 2) + hh), "o0_%d_%d" % (tt, hh))
+                o0t[(tt, hh)] = t0
+                hs = slice(8 * hh, 8 * hh + 8)
+                nc.gpsimd.tensor_tensor(
+                    out=t0[:, :, 128:160], in0=ya[:, 0, hs, :], in1=yb[:, 1, hs, :], op=ALU.subtract
+                )
+                nc.gpsimd.tensor_tensor(out=t0[:, :, 160:192], in0=ya[:, 1, hs, :], in1=yb[:, 0, hs, :], op=ALU.add)
 
         def ku_tiles(tt):
             bi, si = divmod(tt, 8)
             rows = slice(si * P, (si + 1) * P)
             for i in range(4):
                 hh = i // 2
-                if i % 2 == 0:
-                    o0t[(tt, hh)] = sbt([P, 8, 192], F32, "xc%d" % (12 + 2 * (tt % 2) + hh), "o0_%d_%d" % (tt, hh))
                 need(4 + i)
                 o = mm2(tt, 4 + i)
                 h0 = (i % 2) * 4
@@ -448,7 +463,6 @@ def tile_multiheadlatentattention_pa_l_kernel(
                     op=ALU.add,
                 )
                 if i % 2 == 1:
-                    rope_sum(tt, hh)
                     nc.sync.dma_start(
                         out=out_0[bi, 8 * hh : 8 * hh + 8, rows, :].rearrange("h s d -> s h d"), in_=o0t[(tt, hh)]
                     )

@@ -19,8 +19,10 @@ P = 128
 PI = 3.141592653589793
 NG = 4
 NRAW = 3
-SORT_LO, SORT_HI = 40, 40
-NV_MID = 2
+SORT_LO, SORT_HI = 8, 30
+NV_MID = 0
+NV_LAST = 0
+SORT_ENG = "v"
 EARLY = 30
 LATE_EVERY = 2
 FIRST = 8
@@ -78,9 +80,12 @@ def tile_multiheadlatentattention_pa_l_kernel(
             xraw[n] = t
 
         def sort_x(n):
-            t = sbt([P, 8, 2, P], F32, "xc%d" % (12 + n % 4), "xsort%d" % n)
+            t = sbt([P, 8, 2, P], F32, "xc%d" % (12 + n % 4 if n < 22 else 14 + n % 2), "xsort%d" % n)
             words = xraw[n].rearrange("p a k -> p (a k)").bitcast(F32)
-            nc.scalar.copy(out=t, in_=words.rearrange("p (b w u) -> p b u w", b=8, u=2))
+            if SORT_ENG == "v":
+                nc.vector.tensor_copy(out=t, in_=words.rearrange("p (b w u) -> p b u w", b=8, u=2))
+            else:
+                nc.scalar.copy(out=t, in_=words.rearrange("p (b w u) -> p b u w", b=8, u=2))
             xsorted[n] = t
 
         def transposes(n):
@@ -213,8 +218,8 @@ def tile_multiheadlatentattention_pa_l_kernel(
                 elif U % 4 == 0:
                     when.append((U // 4 - 1) * 32 + 8 + 2 * r)
                 else:
-                    V = U - 5
-                    when.append((V // 4) * 32 + 24 + 2 * (V % 4) + 2 + r // 2)
+                    k = 4 * (U % 4 - 1) + r
+                    when.append((U // 4 - 1) * 32 + 26 + (k if k < 4 else 4 + (k - 4) // 2))
         for m in range(40):
             when.append(98 + m if m < EARLY else 1000)
 
@@ -354,7 +359,7 @@ def tile_multiheadlatentattention_pa_l_kernel(
             if sig + 2 < 32:
                 if SORT_LO <= sig + 3 < SORT_HI:
                     sort_x(sig + 3)
-                x_front(sig + 2, 1 if (sig < 8 or sig >= 24) else NV_MID)
+                x_front(sig + 2, 1 if sig < 8 else (NV_LAST if sig >= 24 else NV_MID))
                 for n in range(4, 32):
                     if (n - 5 if (SORT_LO <= n - 2 < SORT_HI or n in (8, 9)) else n - 4) == sig:
                         load_x(n)

@@ -205,7 +205,7 @@ def tile_multiheadlatentattention_pa_l_kernel(
             st["ic"] = k + 1
             if st["q"] < k:
                 flush_q()
-            if st["dma"] <= k + NRAW:
+            if st["dma"] <= k + NRAW and k >= 16:
                 job_dma()
 
         when = []
@@ -216,7 +216,7 @@ def tile_multiheadlatentattention_pa_l_kernel(
                 elif U < 4:
                     when.append((4 * U + r - 4) // 2)
                 elif U % 4 == 0:
-                    when.append((U // 4 - 1) * 32 + 8 + 2 * r)
+                    when.append((U // 4 - 1) * 32 + 12 + 2 * r)
                 else:
                     k = 4 * (U % 4 - 1) + r
                     when.append((U // 4 - 1) * 32 + 26 + (k if k < 4 else 4 + (k - 4) // 2))
@@ -373,6 +373,9 @@ def tile_multiheadlatentattention_pa_l_kernel(
             run_jobs(sig, "vs", 8)
             c_quant()
             flush_q()
+            if sig == 9:
+                for i in range(NRAW):
+                    job_dma()
             if sig == 5:
                 nc.vector.tensor_copy(out=bk, in_=bkb.rearrange("p g t -> p (g t)"))
             if sig == 33:
@@ -391,23 +394,26 @@ def tile_multiheadlatentattention_pa_l_kernel(
         c_quant()
 
         def mm2(tt, i):
-            b = st["bank"] % 8
-            st["bank"] = st["bank"] + 1
-            out = bank(b, [P, 512], "o%d_%d" % (tt, i))
-            assert st["q"] >= 64 + 4 * i + 4
-            codes, plane = units[("u", i)]
+            outs = []
+            for z in range(2):
+                b = st["bank"] % 8
+                st["bank"] = st["bank"] + 1
+                outs.append(bank(b, [P, 512], "o%d_%d" % (tt, i + z)))
+            assert st["q"] >= 64 + 4 * (i + 1) + 4
             cols = slice(tt * P, (tt + 1) * P)
             for r in range(4):
-                nc.tensor.matmul_mx(
-                    out=out,
-                    lhsT=cc[r][:, cols].bitcast(FP8),
-                    lhsT_scale=cp[4 * r : P, cols],
-                    rhs=codes[:, r, :].bitcast(FP8),
-                    rhs_scale=plane[4 * r : P, :],
-                    start=(r == 0),
-                    stop=(r == 3),
-                )
-            return out
+                for z in range(2):
+                    codes, plane = units[("u", i + z)]
+                    nc.tensor.matmul_mx(
+                        out=outs[z],
+                        lhsT=cc[r][:, cols].bitcast(FP8),
+                        lhsT_scale=cp[4 * r : P, cols],
+                        rhs=codes[:, r, :].bitcast(FP8),
+                        rhs_scale=plane[4 * r : P, :],
+                        start=(r == 0),
+                        stop=(r == 3),
+                    )
+            return outs
 
         cos3 = tabs["cos"].rearrange("p (s j) -> p s j", j=32)
         sin3 = tabs["sin"].rearrange("p (s j) -> p s j", j=32)
@@ -426,9 +432,10 @@ def tile_multiheadlatentattention_pa_l_kernel(
         def kr_tiles(tt):
             si = tt % 8
             y = sbt([P, 16, 2, 32], F32, "wc%d" % (2 + tt % 2), "y%d" % tt)
+            need(9)
+            outs = mm2(tt, 8)
             for i in range(2):
-                need(8 + i)
-                o = mm2(tt, 8 + i)
+                o = outs[i]
                 nc.vector.tensor_tensor(
                     out=y[:, 8 * i : 8 * i + 8].rearrange("p h f j -> p h (f j)"),
                     in0=o.rearrange("p (h d) -> p h d", h=8),
@@ -458,8 +465,10 @@ def tile_multiheadlatentattention_pa_l_kernel(
             rows = slice(si * P, (si + 1) * P)
             for i in range(4):
                 hh = i // 2
-                need(4 + i)
-                o = mm2(tt, 4 + i)
+                if i % 2 == 0:
+                    need(5 + i)
+                    outs = mm2(tt, 4 + i)
+                o = outs[i % 2]
                 h0 = (i % 2) * 4
                 nc.vector.tensor_tensor(
                     out=o0t[(tt, hh)][:, h0 : h0 + 4, 0:128],
@@ -479,8 +488,10 @@ def tile_multiheadlatentattention_pa_l_kernel(
             if i == 0:
                 o1t[tt] = sbt([P, 16, 128], F32, "wc%d" % (0 if tt % 2 == 0 else 4), "o1_%d" % tt)
             o1 = o1t[tt]
-            need(i)
-            o = mm2(tt, i)
+            if i % 2 == 0:
+                need(i + 1)
+                o1t["outs"] = mm2(tt, i)
+            o = o1t["outs"][i % 2]
             nc.vector.tensor_tensor(
                 out=o1[:, 4 * i : 4 * i + 4, :],
                 in0=o.rearrange("p (h d) -> p h d", h=4),

@@ -205,7 +205,7 @@ def tile_multiheadlatentattention_pa_l_kernel(
             st["ic"] = k + 1
             if st["q"] < k:
                 flush_q()
-            if st["dma"] <= k + NRAW and k >= 16:
+            if st["dma"] <= k + NRAW:
                 job_dma()
 
         when = []
@@ -216,7 +216,7 @@ def tile_multiheadlatentattention_pa_l_kernel(
                 elif U < 4:
                     when.append((4 * U + r - 4) // 2)
                 elif U % 4 == 0:
-                    when.append((U // 4 - 1) * 32 + 12 + 2 * r)
+                    when.append((U // 4 - 1) * 32 + 8 + 2 * r)
                 else:
                     k = 4 * (U % 4 - 1) + r
                     when.append((U // 4 - 1) * 32 + 26 + (k if k < 4 else 4 + (k - 4) // 2))
@@ -241,12 +241,17 @@ def tile_multiheadlatentattention_pa_l_kernel(
             if j == 0:
                 for t in range(4):
                     acc[t] = bank(base + t, [P, 512], "acc%d_%d" % (s, t))
-            for kl in range(2):
-                kp = 2 * j + kl
-                q, rr = kp // 4, kp % 4
-                assert st["q"] >= 4 * (4 * g + q) + 4
-                codes, plane = units[("w", 4 * g + q)]
-                for t in range(4):
+            if g == 0:
+                kps = [2 * j, 2 * j + 1]
+            elif j % 2 == 1:
+                kps = [2 * j - 2, 2 * j - 1, 2 * j, 2 * j + 1]
+            else:
+                kps = []
+            for t in range(4):
+                for kp in kps:
+                    q, rr = kp // 4, kp % 4
+                    assert st["q"] >= 4 * (4 * g + q) + 4
+                    codes, plane = units[("w", 4 * g + q)]
                     cols = slice(t * P, (t + 1) * P)
                     nc.tensor.matmul_mx(
                         out=acc[t],
@@ -373,9 +378,6 @@ def tile_multiheadlatentattention_pa_l_kernel(
             run_jobs(sig, "vs", 8)
             c_quant()
             flush_q()
-            if sig == 9:
-                for i in range(NRAW):
-                    job_dma()
             if sig == 5:
                 nc.vector.tensor_copy(out=bk, in_=bkb.rearrange("p g t -> p (g t)"))
             if sig == 33:
@@ -394,26 +396,23 @@ def tile_multiheadlatentattention_pa_l_kernel(
         c_quant()
 
         def mm2(tt, i):
-            outs = []
-            for z in range(2):
-                b = st["bank"] % 8
-                st["bank"] = st["bank"] + 1
-                outs.append(bank(b, [P, 512], "o%d_%d" % (tt, i + z)))
-            assert st["q"] >= 64 + 4 * (i + 1) + 4
+            b = st["bank"] % 8
+            st["bank"] = st["bank"] + 1
+            out = bank(b, [P, 512], "o%d_%d" % (tt, i))
+            assert st["q"] >= 64 + 4 * i + 4
+            codes, plane = units[("u", i)]
             cols = slice(tt * P, (tt + 1) * P)
             for r in range(4):
-                for z in range(2):
-                    codes, plane = units[("u", i + z)]
-                    nc.tensor.matmul_mx(
-                        out=outs[z],
-                        lhsT=cc[r][:, cols].bitcast(FP8),
-                        lhsT_scale=cp[4 * r : P, cols],
-                        rhs=codes[:, r, :].bitcast(FP8),
-                        rhs_scale=plane[4 * r : P, :],
-                        start=(r == 0),
-                        stop=(r == 3),
-                    )
-            return outs
+                nc.tensor.matmul_mx(
+                    out=out,
+                    lhsT=cc[r][:, cols].bitcast(FP8),
+                    lhsT_scale=cp[4 * r : P, cols],
+                    rhs=codes[:, r, :].bitcast(FP8),
+                    rhs_scale=plane[4 * r : P, :],
+                    start=(r == 0),
+                    stop=(r == 3),
+                )
+            return out
 
         cos3 = tabs["cos"].rearrange("p (s j) -> p s j", j=32)
         sin3 = tabs["sin"].rearrange("p (s j) -> p s j", j=32)
@@ -432,10 +431,9 @@ def tile_multiheadlatentattention_pa_l_kernel(
         def kr_tiles(tt):
             si = tt % 8
             y = sbt([P, 16, 2, 32], F32, "wc%d" % (2 + tt % 2), "y%d" % tt)
-            need(9)
-            outs = mm2(tt, 8)
             for i in range(2):
-                o = outs[i]
+                need(8 + i)
+                o = mm2(tt, 8 + i)
                 nc.vector.tensor_tensor(
                     out=y[:, 8 * i : 8 * i + 8].rearrange("p h f j -> p h (f j)"),
                     in0=o.rearrange("p (h d) -> p h d", h=8),
@@ -465,10 +463,8 @@ def tile_multiheadlatentattention_pa_l_kernel(
             rows = slice(si * P, (si + 1) * P)
             for i in range(4):
                 hh = i // 2
-                if i % 2 == 0:
-                    need(5 + i)
-                    outs = mm2(tt, 4 + i)
-                o = outs[i % 2]
+                need(4 + i)
+                o = mm2(tt, 4 + i)
                 h0 = (i % 2) * 4
                 nc.vector.tensor_tensor(
                     out=o0t[(tt, hh)][:, h0 : h0 + 4, 0:128],
@@ -488,10 +484,8 @@ def tile_multiheadlatentattention_pa_l_kernel(
             if i == 0:
                 o1t[tt] = sbt([P, 16, 128], F32, "wc%d" % (0 if tt % 2 == 0 else 4), "o1_%d" % tt)
             o1 = o1t[tt]
-            if i % 2 == 0:
-                need(i + 1)
-                o1t["outs"] = mm2(tt, i)
-            o = o1t["outs"][i % 2]
+            need(i)
+            o = mm2(tt, i)
             nc.vector.tensor_tensor(
                 out=o1[:, 4 * i : 4 * i + 4, :],
                 in0=o.rearrange("p (h d) -> p h d", h=4),

from contextlib import ExitStack
import math

import concourse.mybir as mybir
from concourse.masks import make_identity

F32 = mybir.dt.float32
BF16 = mybir.dt.bfloat16
U32 = mybir.dt.uint32
U8 = mybir.dt.uint8
I32 = mybir.dt.int32
FP8 = mybir.dt.float8_e4m3fn_x4
ALU = mybir.AluOpType
ACT = mybir.ActivationFunctionType

FLOPS = 2 * 2048 * 8192 * 2048 + 2 * 2048 * 2048 * 5120

P = 128
PI = 3.141592653589793
NG = 4
NRAW = 3
SORT_LO, SORT_HI = 8, 30
NV_MID = 0
NV_LAST = 0
SORT_ENG = "v"
EARLY = 30
LATE_EVERY = 2
FIRST = 8


def turn_constants():
    heads, rests = [], []
    for j in range(32):
        f = math.exp(-math.log(10000.0) * j / 32.0) / (2.0 * PI)
        s = 0
        for i in range(40):
            if f * (2.0 ** s) < 2048.0:
                s = s + 1
        head = int(f * (2.0 ** s)) / (2.0 ** s)
        heads.append(head)
        rests.append(f - head)
    return heads, rests


def tile_multiheadlatentattention_pa_l_kernel(
    tc, x, W_kvd, b_kvd, W_ku, b_ku, W_vu, b_vu, W_kr, b_kr, out_0, out_1
):
    nc = tc.nc
    xf = x.flatten_outer_dims()
    with ExitStack() as ctx:
        sb = ctx.enter_context(tc.tile_pool(name="sb", bufs=1))
        ps = ctx.enter_context(tc.psum_pool(name="ps", bufs=1))
        ctx.enter_context(tc.manual_schedule())

        def sbt(shape, dtype, tag, label):
            return sb.tile(shape, dtype, name=label, tag=tag, align_bytes=64)

        def bank(b, shape, label):
            return ps.tile(shape, F32, name=label, tag="bank%d" % b)

        st = {"gx": 0, "gw": 0, "dma": 0, "ic": 0, "q": 0, "bank": 4, "tile": 0}

        def granule(kind, label):
            i = st[kind] % NG
            st[kind] = st[kind] + 1
            return sbt([P, 1024], BF16, "%s%d" % (kind, i), label)

        xraw, tpb, xg, xcu, xpu, xsorted = {}, {}, {}, {}, {}, {}

        def load_x(n):
            tb, j = divmod(n, 8)
            tag = ("cc1", "cc2", "xc6", "xc7")[n % 4] if n < 8 else "cc%d" % (1 + n % 2)
            t = sbt([P, 4, 1024], BF16, tag, "xraw%d" % n)
            src = xf[tb * 512 : (tb + 1) * 512, j * 1024 : (j + 1) * 1024].rearrange("(a p) k -> p a k", p=P)
            if n == 0:
                for a in range(4):
                    nc.sync.dma_start(out=t[:, a, :], in_=src[:, a, :])
            else:
                nc.sync.dma_start(out=t, in_=src)
            xraw[n] = t

        def sort_x(n):
            t = sbt([P, 8, 2, P], F32, "xc%d" % (12 + n % 4 if n < 22 else 14 + n % 2), "xsort%d" % n)
            words = xraw[n].rearrange("p a k -> p (a k)").bitcast(F32)
            if SORT_ENG == "v":
                nc.vector.tensor_copy(out=t, in_=words.rearrange("p (b w u) -> p b u w", b=8, u=2))
            else:
                nc.scalar.copy(out=t, in_=words.rearrange("p (b w u) -> p b u w", b=8, u=2))
            xsorted[n] = t

        def transposes(n):
            words = xraw[n].rearrange("p a k -> p (a k)").bitcast(F32)
            for kl in range(2):
                for h in range(2):
                    b = bank(4 + 2 * kl + h, [P, 2, 2, P], "tp%d_%d%d" % (n, kl, h))
                    tpb[(n, kl, h)] = b
                    for a2 in range(2):
                        for u in range(2):
                            if n in xsorted:
                                nc.tensor.transpose(b[:, a2, u, :], xsorted[n][:, (2 * h + a2) * 2 + kl, u, :], ident)
                            else:
                                base = (2 * h + a2) * 512 + kl * 256 + u
                                nc.tensor.transpose(b[:, a2, u, :], words[:, base : base + 255 : 2], ident)

        def copy_out(n, kl, h, eng):
            g = granule("gx", "xg%d_%d%d" % (n, kl, h))
            dst = g.bitcast(F32).rearrange("p (a r u) -> p a r u", a=2, u=2)
            src = tpb[(n, kl, h)].rearrange("p a u r -> p a r u")
            if eng == "v":
                nc.vector.tensor_copy(out=dst, in_=src)
            else:
                nc.scalar.copy(out=dst, in_=src)
            xg[(n, kl, h)] = g

        def quant_x(n, kl, h):
            tb, j = divmod(n, 8)
            kp = 2 * j + kl
            i, r = tb * 4 + kp // 4, kp % 4
            if i not in xcu:
                xcu[i] = sbt([P, 4, 512], U32, "xc%d" % i, "xcodes%d" % i)
                xpu[i] = sbt([P, 512], U8, "xp%d" % i, "xplane%d" % i)
            cols = slice(h * 256, (h + 1) * 256)
            nc.vector.quantize_mx(
                out=xcu[i][:, r, cols].bitcast(FP8), scales=xpu[i][4 * r : P, cols], in_=xg[(n, kl, h)]
            )

        jobs = []
        for U in range(16):
            for r in range(4):
                kp = 4 * (U % 4) + r
                g = U // 4
                jobs.append(("w", U, r, W_kvd[kp * 512 : (kp + 1) * 512, g * 512 : (g + 1) * 512]))
        for i in range(10):
            if i < 4:
                src, c0 = W_vu, i
            elif i < 8:
                src, c0 = W_ku, i - 4
            else:
                src, c0 = W_kr, i - 8
            for r in range(4):
                jobs.append(("u", i, r, src[r * 512 : (r + 1) * 512, c0 * 512 : (c0 + 1) * 512]))
        wraw, wg, units, wpair = {}, {}, {}, {}

        def job_dma():
            k = st["dma"]
            if k >= len(jobs):
                return
            st["dma"] = k + 1
            if k < 16:
                if k % 2 == 0:
                    wpair[k // 2] = sbt([P, 2, 4, 512], BF16, "xc%d" % (8 + k // 2), "rawpair%d" % (k // 2))
                t = wpair[k // 2][:, k % 2]
            else:
                t = sbt([P, 4, 512], BF16, "raw%d" % (k % NRAW), "raw_j%d" % k)
            nc.sync.dma_start(out=t, in_=jobs[k][3].rearrange("(p j) c -> p j c", j=4))
            wraw[k] = t

        def job_ic(k, engs):
            kind = jobs[k][0]
            for h in range(2):
                g = granule("gw", "wg%d_%d" % (k, h))
                if kind == "w":
                    src = wraw[k].rearrange("p j (m t) -> p t m j", t=4)[:, 2 * h : 2 * h + 2]
                    dst = g.rearrange("p (t m j) -> p t m j", t=2, j=4)
                else:
                    src = wraw[k][:, :, h * 256 : (h + 1) * 256].rearrange("p j c -> p c j")
                    dst = g.rearrange("p (c j) -> p c j", j=4)
                if engs[h] == "v":
                    nc.vector.tensor_copy(out=dst, in_=src)
                else:
                    nc.scalar.copy(out=dst, in_=src)
                wg[(k, h)] = g

        def job_q(k):
            kind, U, r = jobs[k][0], jobs[k][1], jobs[k][2]
            if r == 0:
                if kind == "w":
                    units[(kind, U)] = (
                        sbt([P, 4, 512], U32, "wc%d" % (U % 5), "wcodes%d" % U),
                        sbt([P, 512], U8, "wp%d" % (U % 5), "wplane%d" % U),
                    )
                else:
                    units[(kind, U)] = (
                        sbt([P, 4, 512], U32, "xc%d" % U, "ucodes%d" % U),
                        sbt([P, 512], U8, "xp%d" % U, "uplane%d" % U),
                    )
            codes, plane = units[(kind, U)]
            for h in range(2):
                cols = slice(h * 256, (h + 1) * 256)
                nc.vector.quantize_mx(
                    out=codes[:, r, cols].bitcast(FP8), scales=plane[4 * r : P, cols], in_=wg[(k, h)]
                )

        def flush_q():
            if st["q"] < st["ic"]:
                job_q(st["q"])
                st["q"] = st["q"] + 1

        def advance(engs):
            k = st["ic"]
            if k >= len(jobs):
                flush_q()
                return
            job_ic(k, engs)
            st["ic"] = k + 1
            if st["q"] < k:
                flush_q()
            if st["dma"] <= k + NRAW:
                job_dma()

        when = []
        for U in range(16):
            for r in range(4):
                if U == 0:
                    when.append(-1)
                elif U < 4:
                    when.append((4 * U + r - 4) // 2)
                elif U % 4 == 0:
                    when.append((U // 4 - 1) * 32 + 8 + 2 * r)
                else:
                    k = 4 * (U % 4 - 1) + r
                    when.append((U // 4 - 1) * 32 + 26 + (k if k < 4 else 4 + (k - 4) // 2))
        for m in range(40):
            when.append(98 + m if m < EARLY else 1000)

        def run_jobs(sig, engs, most):
            did = 0
            for i in range(most):
                if st["ic"] < len(jobs) and when[st["ic"]] <= sig:
                    advance(engs)
                    did = did + 1
            return did

        acc, cc, cwork = {}, {}, []

        def mm1(sig):
            g, r = divmod(sig, 32)
            tb, j = divmod(r, 8)
            s = g * 4 + tb
            base = 0 if g == 0 else 4 * ((s + 1) % 2)
            if j == 0:
                for t in range(4):
                    acc[t] = bank(base + t, [P, 512], "acc%d_%d" % (s, t))
            if g == 0:
                kps = [2 * j, 2 * j + 1]
            elif j % 2 == 1:
                kps = [2 * j - 2, 2 * j - 1, 2 * j, 2 * j + 1]
            else:
                kps = []
            for t in range(4):
                for kp in kps:
                    q, rr = kp // 4, kp % 4
                    assert st["q"] >= 4 * (4 * g + q) + 4
                    codes, plane = units[("w", 4 * g + q)]
                    cols = slice(t * P, (t + 1) * P)
                    nc.tensor.matmul_mx(
                        out=acc[t],
                        lhsT=codes[:, rr, cols].bitcast(FP8),
                        lhsT_scale=plane[4 * rr : P, cols],
                        rhs=xcu[tb * 4 + q][:, rr, :].bitcast(FP8),
                        rhs_scale=xpu[tb * 4 + q][4 * rr : P, :],
                        start=(kp == 0),
                        stop=(kp == 15),
                    )

        def evac(g, tb):
            cbf = sbt([P, 4, 512], BF16, "cbf", "cbf%d_%d" % (g, tb))
            for t in range(4):
                col = bk[:, 4 * g + t : 4 * g + t + 1]
                if t % 2 == 0:
                    nc.scalar.activation(out=cbf[:, t, :], in_=acc[t], func=ACT.Identity, bias=col, scale=1.0)
                else:
                    nc.vector.tensor_scalar(out=cbf[:, t, :], in0=acc[t], scalar1=col, scalar2=None, op0=ALU.add)
            cwork.append((g, tb, cbf))

        def c_quant():
            if len(cwork) == 0:
                return
            flush_q()
            g, tb, cbf = cwork.pop(0)
            if tb == 0:
                cc[g] = sbt([P, 2048], U32, ("cc%d" % g) if g < 3 else "wc1", "ccodes%d" % g)
            gs = []
            for h in range(2):
                gr = granule("gw", "cg%d_%d_%d" % (g, tb, h))
                nc.vector.tensor_copy(
                    out=gr.rearrange("p (n t) -> p n t", t=4),
                    in_=cbf[:, :, h * 256 : (h + 1) * 256].rearrange("p t n -> p n t"),
                )
                gs.append(gr)
            for h in range(2):
                cols = slice(tb * 512 + h * 256, tb * 512 + (h + 1) * 256)
                nc.vector.quantize_mx(out=cc[g][:, cols].bitcast(FP8), scales=cp[4 * g : P, cols], in_=gs[h])

        tabs = {}

        def rope_part1():
            tmp = sbt([P, 2048], F32, "cc2", "ropetmp")
            tabs["tmp"] = tmp
            posi = tmp[:, 2040:2048].bitcast(I32)
            posf = tmp[:, 2032:2040]
            nc.gpsimd.iota(posi, pattern=[[128, 8]], base=0, channel_multiplier=1)
            nc.vector.tensor_copy(out=posf, in_=posi)
            heads, rests = turn_constants()
            th = tmp[:, 0:256].rearrange("p (s j) -> p s j", j=32)
            tl = tmp[:, 256:512].rearrange("p (s j) -> p s j", j=32)
            for j in range(32):
                nc.gpsimd.tensor_scalar(
                    out=th[:, :, j], in0=posf, scalar1=heads[j], scalar2=0.0, op0=ALU.mult, op1=ALU.add
                )
                nc.gpsimd.tensor_scalar(
                    out=tl[:, :, j], in0=posf, scalar1=rests[j], scalar2=0.0, op0=ALU.mult, op1=ALU.add
                )

        def rope_part2():
            tmp = tabs["tmp"]
            th, tl = tmp[:, 0:256], tmp[:, 256:512]
            ni = tmp[:, 512:768].bitcast(I32)
            nf, r1, r2, rc = [tmp[:, 768 + 256 * i : 1024 + 256 * i] for i in range(4)]
            ws, wc = th, tl
            nc.vector.tensor_copy(out=ni, in_=th)
            nc.vector.tensor_copy(out=nf, in_=ni)
            nc.vector.tensor_tensor(out=r1, in0=th, in1=nf, op=ALU.subtract)
            nc.vector.tensor_tensor(out=r2, in0=r1, in1=tl, op=ALU.add)
            nc.vector.tensor_scalar(out=rc, in0=r2, scalar1=0.25, scalar2=None, op0=ALU.add)
            nc.vector.scalar_tensor_tensor(out=ws, in0=r2, scalar=0.5, in1=r2, op0=ALU.is_gt, op1=ALU.subtract)
            nc.vector.scalar_tensor_tensor(out=wc, in0=rc, scalar=0.5, in1=rc, op0=ALU.is_gt, op1=ALU.subtract)
            tab = sbt([P, 512], F32, "gx0", "ropetab")
            tabs["sin"], tabs["cos"] = tab[:, 0:256], tab[:, 256:512]
            nc.scalar.activation(out=tabs["sin"], in_=ws, func=ACT.Sin, scale=-2.0 * PI)
            nc.scalar.activation(out=tabs["cos"], in_=wc, func=ACT.Sin, scale=-2.0 * PI)

        ident = sbt([P, P], F32, "ident", "ident")
        make_identity(nc, ident)
        bkb = sbt([P, 4, 4], BF16, "bkb", "bkb")
        bk = sbt([P, 16], F32, "bk", "bk")
        cp = sbt([P, 2048], U8, "cp", "cplane")

        def x_front(n, nv):
            transposes(n)
            for i in range(4):
                copy_out(n, i // 2, i % 2, "v" if i < nv else "s")

        def x_back(n):
            for i in (3, 0, 2, 1):
                quant_x(n, i // 2, i % 2)

        for n in range(4):
            load_x(n)
            job_dma()
            job_dma()
        nc.sync.dma_start(out=bkb, in_=b_kvd.rearrange("(g p t) -> p g t", p=P, t=4))
        x_front(0, 1)
        advance("vs")
        advance("vs")
        x_back(0)
        x_front(1, 1)
        advance("vs")
        advance("vs")
        x_back(1)
        flush_q()

        for sig in range(128):
            if sig + 2 < 32:
                if SORT_LO <= sig + 3 < SORT_HI:
                    sort_x(sig + 3)
                x_front(sig + 2, 1 if sig < 8 else (NV_LAST if sig >= 24 else NV_MID))
                for n in range(4, 32):
                    if (n - 5 if (SORT_LO <= n - 2 < SORT_HI or n in (8, 9)) else n - 4) == sig:
                        load_x(n)
                if sig < 4:
                    job_dma()
                    job_dma()
            if sig < 28:
                run_jobs(sig, "vs", 1)
            if sig + 2 < 32:
                x_back(sig + 2)
            run_jobs(sig, "vs", 8)
            c_quant()
            flush_q()
            if sig == 5:
                nc.vector.tensor_copy(out=bk, in_=bkb.rearrange("p g t -> p (g t)"))
            if sig == 33:
                rope_part1()
            if sig == 46:
                rope_part2()
            if sig == 120:
                bkv = sbt([P, 4096], BF16, "xc10", "bias_kv")
                bkr = sbt([P, 1024], BF16, "xc11", "bias_kr")
                nc.sync.dma_start(out=bkr, in_=b_kr.partition_broadcast(P))
                nc.sync.dma_start(out=bkv[:, 0:2048], in_=b_ku.partition_broadcast(P))
                nc.sync.dma_start(out=bkv[:, 2048:4096], in_=b_vu.partition_broadcast(P))
            mm1(sig)
            if sig % 8 == 7:
                evac(sig // 32, (sig % 32) // 8)
        c_quant()

        def mm2(tt, i):
            b = st["bank"] % 8
            st["bank"] = st["bank"] + 1
            out = bank(b, [P, 512], "o%d_%d" % (tt, i))
            assert st["q"] >= 64 + 4 * i + 4
            codes, plane = units[("u", i)]
            cols = slice(tt * P, (tt + 1) * P)
            for r in range(4):
                nc.tensor.matmul_mx(
                    out=out,
                    lhsT=cc[r][:, cols].bitcast(FP8),
                    lhsT_scale=cp[4 * r : P, cols],
                    rhs=codes[:, r, :].bitcast(FP8),
                    rhs_scale=plane[4 * r : P, :],
                    start=(r == 0),
                    stop=(r == 3),
                )
            return out

        cos3 = tabs["cos"].rearrange("p (s j) -> p s j", j=32)
        sin3 = tabs["sin"].rearrange("p (s j) -> p s j", j=32)
        o0t, o1t = {}, {}

        def late_jobs():
            st["tile"] = st["tile"] + 1
            if st["tile"] % LATE_EVERY == 0:
                advance("ss")

        def need(i):
            for n in range(48):
                if st["q"] < 64 + 4 * i + 4:
                    advance("ss")

        def kr_tiles(tt):
            si = tt % 8
            y = sbt([P, 16, 2, 32], F32, "wc%d" % (2 + tt % 2), "y%d" % tt)
            for i in range(2):
                need(8 + i)
                o = mm2(tt, 8 + i)
                nc.vector.tensor_tensor(
                    out=y[:, 8 * i : 8 * i + 8].rearrange("p h f j -> p h (f j)"),
                    in0=o.rearrange("p (h d) -> p h d", h=8),
                    in1=bkr[:, i * 512 : (i + 1) * 512].rearrange("p (h d) -> p h d", h=8),
                    op=ALU.add,
                )
                late_jobs()
            ya = sbt([P, 32, 2, 16], F32, "raw0" if tt % 2 == 0 else "raw2", "ycos%d" % tt)
            yb = sbt([P, 32, 2, 16], F32, "raw1" if tt % 2 == 0 else "cbf", "ysin%d" % tt)
            yv = y.rearrange("p h f j -> p j f h")
            for j in range(32):
                nc.scalar.activation(out=ya[:, j], in_=yv[:, j], func=ACT.Copy, scale=cos3[:, si, j : j + 1])
                nc.scalar.activation(out=yb[:, j], in_=yv[:, j], func=ACT.Copy, scale=sin3[:, si, j : j + 1])
            ya = ya.rearrange("p j f h -> p f h j")
            yb = yb.rearrange("p j f h -> p f h j")
            for hh in range(2):
                t0 = sbt([P, 8, 192], F32, "xc%d" % (12 + 2 * (tt % 2) + hh), "o0_%d_%d" % (tt, hh))
                o0t[(tt, hh)] = t0
                hs = slice(8 * hh, 8 * hh + 8)
                nc.gpsimd.tensor_tensor(
                    out=t0[:, :, 128:160], in0=ya[:, 0, hs, :], in1=yb[:, 1, hs, :], op=ALU.subtract
                )
                nc.gpsimd.tensor_tensor(out=t0[:, :, 160:192], in0=ya[:, 1, hs, :], in1=yb[:, 0, hs, :], op=ALU.add)

        def ku_tiles(tt):
            bi, si = divmod(tt, 8)
            rows = slice(si * P, (si + 1) * P)
            for i in range(4):
                hh = i // 2
                need(4 + i)
                o = mm2(tt, 4 + i)
                h0 = (i % 2) * 4
                nc.vector.tensor_tensor(
                    out=o0t[(tt, hh)][:, h0 : h0 + 4, 0:128],
                    in0=o.rearrange("p (h d) -> p h d", h=4),
                    in1=bkv[:, i * 512 : (i + 1) * 512].rearrange("p (h d) -> p h d", h=4),
                    op=ALU.add,
                )
                if i % 2 == 1:
                    nc.sync.dma_start(
                        out=out_0[bi, 8 * hh : 8 * hh + 8, rows, :].rearrange("h s d -> s h d"), in_=o0t[(tt, hh)]
                    )
                late_jobs()

        def vu_tile(tt, i):
            bi, si = divmod(tt, 8)
            rows = slice(si * P, (si + 1) * P)
            if i == 0:
                o1t[tt] = sbt([P, 16, 128], F32, "wc%d" % (0 if tt % 2 == 0 else 4), "o1_%d" % tt)
            o1 = o1t[tt]
            need(i)
            o = mm2(tt, i)
            nc.vector.tensor_tensor(
                out=o1[:, 4 * i : 4 * i + 4, :],
                in0=o.rearrange("p (h d) -> p h d", h=4),
                in1=bkv[:, 2048 + i * 512 : 2048 + (i + 1) * 512].rearrange("p (h d) -> p h d", h=4),
                op=ALU.add,
            )
            if tt == 15:
                nc.sync.dma_start(
                    out=out_1[bi, 4 * i : 4 * i + 4, rows, :].rearrange("h s d -> s h d"),
                    in_=o1[:, 4 * i : 4 * i + 4, :],
                )
            elif i == 3:
                nc.sync.dma_start(out=out_1[bi, :, rows, :].rearrange("h s d -> s h d"), in_=o1)
            late_jobs()

        for tt in range(FIRST):
            for i in range(4):
                vu_tile(tt, i)
        rest = [(tt, i) for tt in range(FIRST, 16) for i in range(4)]
        kr_tiles(0)
        for n in range(16):
            ku_tiles(n)
            if n + 1 < 16:
                kr_tiles(n + 1)
            for m in range(((n + 1) * (16 - FIRST)) // 4 - (n * (16 - FIRST)) // 4):
                tt, i = rest.pop(0)
                vu_tile(tt, i)
